import numpy as np
import ml_dtypes


def mxq(x, axis, fmt="e4m3"):
    dtype, down = {"e4m3": (ml_dtypes.float8_e4m3fn, 7), "e5m2": (ml_dtypes.float8_e5m2, 14)}[fmt]
    v = np.moveaxis(np.asarray(x, np.float32).astype(ml_dtypes.bfloat16).astype(np.float64), axis, -1)
    blocks = v.reshape(v.shape[:-1] + (-1, 32))
    amax = np.abs(blocks).max(-1, keepdims=True)
    byte = np.maximum(np.where(amax > 0, np.frexp(amax)[1] - 1 + 127, 0) - down, 1)
    scale = np.exp2(byte - 127.0)
    codes = (blocks / scale).astype(np.float32).astype(dtype).astype(np.float64)
    return np.moveaxis((codes * scale).reshape(v.shape), -1, axis)


WIDE = False


def mx_kscale(k):
    if not WIDE:
        return np.ones(k)
    levels = np.array([10, -10, 5, -5, 0])
    a = np.random.permutation(np.resize(levels, k // 512 * 4)).reshape(k // 512, 4)
    idx = np.arange(k)
    return np.exp2(a[idx // 512, idx % 128 // 32])


BF16 = ml_dtypes.bfloat16


def bf(x):
    return np.asarray(x, np.float32).astype(BF16)


def f64(x):
    return np.asarray(x).astype(np.float64)


B, C, ROWS, COLS, H, W = 512, 16, 32, 32, 16, 32
K = ROWS * COLS
N = H * W
DENSITY = 0.1


def setup_inputs():
    s = mx_kscale(K)
    image = np.random.standard_normal((B, C, K)) * s
    votes = (np.random.random_sample((K, N)) < DENSITY) * (1.0 + 0.25 * np.random.standard_normal((K, N))) / s[:, None]
    return {"image": bf(image.reshape(B, C, ROWS, COLS)), "vote_index": bf(votes.reshape(ROWS, COLS, H, W))}


def reference(image, vote_index):
    rows, cols, h, w = vote_index.shape
    b, c = image.shape[0], image.shape[1]
    V = f64(vote_index).reshape(rows * cols, h * w)
    x = np.maximum(f64(image).reshape(b * c, rows * cols), 0.0)
    ht = (mxq(x, 1, "e4m3") @ mxq(V, 0, "e4m3")) / cols
    return ht.reshape(b, c, h, w)

@@ -1,0 +1,181 @@
+from contextlib import ExitStack
+
+import concourse.mybir as mybir
+from concourse.masks import make_identity
+
+BF16 = mybir.dt.bfloat16
+F32 = mybir.dt.float32
+U32 = mybir.dt.uint32
+U8 = mybir.dt.uint8
+FP8X4 = mybir.dt.float8_e4m3fn_x4
+COPY = mybir.ActivationFunctionType.Copy
+
+P = 128
+M = 8192
+K = 1024
+N = 512
+FLOPS = 2 * M * K * N
+
+MT = M // P
+GROUP = 4
+NG = MT // GROUP
+SLOT = 8
+LOADS = [2, 2, 4, 4, 4, 8, 8, 8, 8, 8, 8]
+STORES = [8, 8, 8, 8, 8, 8, 8, 4, 2, 2]
+
+
+def tile_ht_t_kernel(tc, image, vote_index, out):
+    nc = tc.nc
+    x_dram = image.rearrange("(p s) c r w -> p (s c r w)", s=4)
+    o_dram = out.rearrange("(p s) c h w -> p (s c h w)", s=4)
+    v_dram = vote_index.rearrange("r w h v -> (r w) (h v)").rearrange(
+        "(j q e) n -> q j (e n)", j=4, e=2
+    )
+    store_ends = {}
+    pos = 0
+    for cnt in STORES:
+        store_ends[pos + cnt] = pos
+        pos += cnt
+
+    with ExitStack() as ctx:
+        const = ctx.enter_context(tc.tile_pool(name="const", bufs=1))
+        io = ctx.enter_context(tc.tile_pool(name="io", bufs=1))
+        work = ctx.enter_context(tc.tile_pool(name="work", bufs=2))
+        tps = ctx.enter_context(tc.psum_pool(name="tps", bufs=1))
+        ops = ctx.enter_context(tc.psum_pool(name="ops", bufs=1))
+        ctx.enter_context(tc.manual_schedule())
+
+        ident = const.tile([P, P], F32, name="ident")
+        make_identity(nc, ident[:])
+
+        x_sb = []
+        for c in range(MT // SLOT):
+            x_sb.append(io.tile([P, SLOT * K], BF16, name="x%d" % c, tag="io%d" % c))
+        o_sb = {}
+        vraw = const.tile([P, 4, 2 * N], BF16, name="vraw")
+        vgrp = const.tile([P, 2, N, 4], BF16, name="vgrp", align_bytes=64)
+        vcodes = const.tile([P, 2 * N], U32, name="vcodes", align_bytes=64)
+        vscl = const.tile([P, 2 * N], U8, name="vscl", align_bytes=64)
+
+        pos = 0
+        for li, cnt in enumerate(LOADS):
+            c = pos // SLOT
+            lo = (pos % SLOT) * K
+            nc.sync.dma_start(
+                out=x_sb[c][:, lo : lo + cnt * K],
+                in_=x_dram[:, pos * K : (pos + cnt) * K],
+            )
+            if li == 0:
+                nc.sync.dma_start(out=vraw[:], in_=v_dram)
+            pos += cnt
+
+        def relu(m0, cnt):
+            c = m0 // SLOT
+            lo = (m0 % SLOT) * K
+            ap = x_sb[c][:, lo : lo + cnt * K]
+            nc.vector.tensor_scalar_max(out=ap, in0=ap, scalar1=0.0)
+
+        def v_regroup(g, eng_copy):
+            src = vraw[:].rearrange("q j (e n) -> q (j e) n", e=2)[:, 4 * g : 4 * g + 4, :]
+            eng_copy(
+                out=vgrp[:, g].rearrange("q (c i) t -> q c t i", i=4),
+                in_=src.rearrange("q t (c i) -> q c t i", i=4),
+            )
+
+        def v_quant(g):
+            nc.vector.quantize_mx(
+                out=vcodes[:, N * g : N * g + N].bitcast(FP8X4),
+                scales=vscl[:, N * g : N * g + N],
+                in_=vgrp[:, g].rearrange("q n t -> q (n t)"),
+            )
+
+        tbs = {}
+        grp = {}
+        cod = {}
+        obs = {}
+
+        def transposes(i):
+            for b in range(GROUP):
+                m = GROUP * i + b
+                tb = tps.tile([P, 4, P], F32, name="tb%d" % b, tag="tb%d" % b)
+                tbs[b] = tb
+                xw = x_sb[m // SLOT][:].bitcast(F32)
+                lo = (m % SLOT) * (K // 2)
+                for j in range(4):
+                    nc.tensor.transpose(
+                        tb[:, j, :], xw[:, lo + P * j : lo + P * j + P], ident[:]
+                    )
+
+        def exits_t(i):
+            grouped = work.tile([P, GROUP * K], BF16, name="grouped", tag="grouped", align_bytes=64)
+            grp[i] = grouped
+            gw = grouped[:].bitcast(F32)
+            for b in range(GROUP):
+                dst = gw[:, 512 * b : 512 * b + 512].rearrange("p (g r u) -> p g r u", g=2, u=2)
+                src = tbs[b][:].rearrange("p (g u) r -> p g r u", u=2)
+                if b % 2 == 0:
+                    nc.vector.tensor_copy(out=dst, in_=src)
+                else:
+                    nc.scalar.copy(out=dst, in_=src)
+
+        def quant(i):
+            codes = work.tile([P, GROUP * 256], U32, name="codes", tag="codes", align_bytes=64)
+            scl = work.tile([P, GROUP * 256], U8, name="scl", tag="scl", align_bytes=64)
+            cod[i] = (codes, scl)
+            nc.vector.quantize_mx(out=codes[:].bitcast(FP8X4), scales=scl[:], in_=grp[i][:])
+
+        def mx(i):
+            codes, scl = cod[i]
+            for b in range(GROUP):
+                ob = ops.tile([P, N], F32, name="ob%d" % b, tag="ob%d" % b)
+                obs[b] = ob
+                for g in range(2):
+                    lo = 256 * b + P * g
+                    nc.tensor.matmul_mx(
+                        out=ob[:],
+                        lhsT=codes[:, lo : lo + P].bitcast(FP8X4),
+                        lhsT_scale=scl[:, lo : lo + P],
+                        rhs=vcodes[:, N * g : N * g + N].bitcast(FP8X4),
+                        rhs_scale=vscl[:, N * g : N * g + N],
+                        start=(g == 0),
+                        stop=(g == 1),
+                    )
+
+        def exits_o(i):
+            for b in range(GROUP):
+                m = GROUP * i + b
+                c = m // SLOT
+                if m % SLOT == 0:
+                    o_sb[c] = io.tile([P, SLOT * N], F32, name="o%d" % c, tag="io%d" % c)
+                lo = (m % SLOT) * N
+                nc.scalar.activation(
+                    out=o_sb[c][:, lo : lo + N], in_=obs[b][:], func=COPY, scale=1.0 / 32.0
+                )
+                if (m + 1) in store_ends:
+                    s0 = store_ends[m + 1]
+                    nc.sync.dma_start(
+                        out=o_dram[:, s0 * N : (m + 1) * N],
+                        in_=o_sb[c][:, (s0 % SLOT) * N : lo + N],
+                    )
+
+        relu(0, 2)
+        v_regroup(0, nc.vector.tensor_copy)
+        v_regroup(1, nc.scalar.copy)
+        v_quant(0)
+        relu(2, 2)
+        transposes(0)
+        exits_t(0)
+        v_quant(1)
+        quant(0)
+        relu(4, 4)
+        relu(8, 4)
+        for i in range(NG):
+            if i + 1 < NG:
+                transposes(i + 1)
+                exits_t(i + 1)
+            if i + 3 < NG:
+                relu(GROUP * (i + 3), GROUP)
+            if i + 1 < NG:
+                quant(i + 1)
+            mx(i)
+            exits_o(i)

@@ -21,7 +21,7 @@ GROUP = 4
 NG = MT // GROUP
 SLOT = 8
 LOADS = [2, 2, 4, 4, 4, 8, 8, 8, 8, 8, 8]
-STORES = [8, 8, 8, 8, 8, 8, 8, 4, 2, 2]
+STORES = [8, 8, 8, 8, 8, 4, 4, 4, 4, 4, 2, 2]
 
 
 def tile_ht_t_kernel(tc, image, vote_index, out):
@@ -57,16 +57,15 @@ def tile_ht_t_kernel(tc, image, vote_index, out):
         vcodes = const.tile([P, 2 * N], U32, name="vcodes", align_bytes=64)
         vscl = const.tile([P, 2 * N], U8, name="vscl", align_bytes=64)
 
+        nc.sync.dma_start(out=vraw[:], in_=v_dram)
         pos = 0
-        for li, cnt in enumerate(LOADS):
+        for cnt in LOADS:
             c = pos // SLOT
             lo = (pos % SLOT) * K
             nc.sync.dma_start(
                 out=x_sb[c][:, lo : lo + cnt * K],
                 in_=x_dram[:, pos * K : (pos + cnt) * K],
             )
-            if li == 0:
-                nc.sync.dma_start(out=vraw[:], in_=v_dram)
             pos += cnt
 
         def relu(m0, cnt):
@@ -106,14 +105,14 @@ def tile_ht_t_kernel(tc, image, vote_index, out):
                         tb[:, j, :], xw[:, lo + P * j : lo + P * j + P], ident[:]
                     )
 
-        def exits_t(i):
+        def exits_t(i, engines):
             grouped = work.tile([P, GROUP * K], BF16, name="grouped", tag="grouped", align_bytes=64)
             grp[i] = grouped
             gw = grouped[:].bitcast(F32)
             for b in range(GROUP):
                 dst = gw[:, 512 * b : 512 * b + 512].rearrange("p (g r u) -> p g r u", g=2, u=2)
                 src = tbs[b][:].rearrange("p (g u) r -> p g r u", u=2)
-                if b % 2 == 0:
+                if engines[b] == "v":
                     nc.vector.tensor_copy(out=dst, in_=src)
                 else:
                     nc.scalar.copy(out=dst, in_=src)
@@ -158,23 +157,22 @@ def tile_ht_t_kernel(tc, image, vote_index, out):
                         in_=o_sb[c][:, (s0 % SLOT) * N : lo + N],
                     )
 
-        relu(0, 2)
         v_regroup(0, nc.vector.tensor_copy)
         v_regroup(1, nc.scalar.copy)
+        relu(0, 2)
         v_quant(0)
         relu(2, 2)
-        transposes(0)
-        exits_t(0)
         v_quant(1)
-        quant(0)
+        transposes(0)
+        exits_t(0, "ssss")
         relu(4, 4)
-        relu(8, 4)
+        quant(0)
         for i in range(NG):
             if i + 1 < NG:
                 transposes(i + 1)
-                exits_t(i + 1)
-            if i + 3 < NG:
-                relu(GROUP * (i + 3), GROUP)
+                exits_t(i + 1, "vsvs")
+            if i + 2 < NG:
+                relu(GROUP * (i + 2), GROUP)
             if i + 1 < NG:
                 quant(i + 1)
             mx(i)

@@ -68,12 +68,6 @@ def tile_ht_t_kernel(tc, image, vote_index, out):
             )
             pos += cnt
 
-        def relu(m0, cnt):
-            c = m0 // SLOT
-            lo = (m0 % SLOT) * K
-            ap = x_sb[c][:, lo : lo + cnt * K]
-            nc.vector.tensor_scalar_max(out=ap, in0=ap, scalar1=0.0)
-
         def v_regroup(g, eng_copy):
             src = vraw[:].rearrange("q j (e n) -> q (j e) n", e=2)[:, 4 * g : 4 * g + 4, :]
             eng_copy(
@@ -96,26 +90,23 @@ def tile_ht_t_kernel(tc, image, vote_index, out):
         def transposes(i):
             for b in range(GROUP):
                 m = GROUP * i + b
-                tb = tps.tile([P, 4, P], F32, name="tb%d" % b, tag="tb%d" % b)
+                tb = tps.tile([P, 4 * P], F32, name="tb%d" % b, tag="tb%d" % b)
                 tbs[b] = tb
                 xw = x_sb[m // SLOT][:].bitcast(F32)
                 lo = (m % SLOT) * (K // 2)
                 for j in range(4):
+                    sl = 2 * (j % 2) + j // 2
                     nc.tensor.transpose(
-                        tb[:, j, :], xw[:, lo + P * j : lo + P * j + P], ident[:]
+                        tb[:, P * sl : P * sl + P], xw[:, lo + P * j : lo + P * j + P], ident[:]
                     )
 
         def exits_t(i, engines):
             grouped = work.tile([P, GROUP * K], BF16, name="grouped", tag="grouped", align_bytes=64)
             grp[i] = grouped
-            gw = grouped[:].bitcast(F32)
             for b in range(GROUP):
-                dst = gw[:, 512 * b : 512 * b + 512].rearrange("p (g r u) -> p g r u", g=2, u=2)
-                src = tbs[b][:].rearrange("p (g u) r -> p g r u", u=2)
-                if engines[b] == "v":
-                    nc.vector.tensor_copy(out=dst, in_=src)
-                else:
-                    nc.scalar.copy(out=dst, in_=src)
+                dst = grouped[:, K * b : K * b + K].rearrange("p (s u e) -> p s u e", u=2, e=2)
+                src = tbs[b][:].bitcast(BF16).rearrange("p (u s e) -> p s u e", u=2, e=2)
+                nc.vector.tensor_scalar_max(out=dst, in0=src, scalar1=0.0)
 
         def quant(i):
             codes = work.tile([P, GROUP * 256], U32, name="codes", tag="codes", align_bytes=64)
@@ -159,21 +150,15 @@ def tile_ht_t_kernel(tc, image, vote_index, out):
 
         v_regroup(0, nc.vector.tensor_copy)
         v_regroup(1, nc.scalar.copy)
-        relu(0, 2)
         v_quant(0)
-        relu(2, 2)
         v_quant(1)
         transposes(0)
-        exits_t(0, "ssss")
-        relu(4, 4)
+        exits_t(0, "vvvv")
         quant(0)
         for i in range(NG):
             if i + 1 < NG:
                 transposes(i + 1)
-                exits_t(i + 1, "vsvs")
-            if i + 2 < NG:
-                relu(GROUP * (i + 2), GROUP)
-            if i + 1 < NG:
+                exits_t(i + 1, "vvvv")
                 quant(i + 1)
             mx(i)
             exits_o(i)

@@ -8,7 +8,7 @@ F32 = mybir.dt.float32
 U32 = mybir.dt.uint32
 U8 = mybir.dt.uint8
 FP8X4 = mybir.dt.float8_e4m3fn_x4
-COPY = mybir.ActivationFunctionType.Copy
+ACT = mybir.ActivationFunctionType
 
 P = 128
 M = 8192
@@ -16,149 +16,148 @@ K = 1024
 N = 512
 FLOPS = 2 * M * K * N
 
-MT = M // P
+PACK = 4
+PASSES = K // (P * PACK)
+WORDS = K // PACK
+ROW_TILES = M // P
 GROUP = 4
-NG = MT // GROUP
+GROUPS = ROW_TILES // GROUP
 SLOT = 8
 LOADS = [2, 2, 4, 4, 4, 8, 8, 8, 8, 8, 8]
 STORES = [8, 8, 8, 8, 8, 4, 4, 4, 4, 4, 2, 2]
+SCALAR_BANK = 1
 
 
 def tile_ht_t_kernel(tc, image, vote_index, out):
     nc = tc.nc
     x_dram = image.rearrange("(p s) c r w -> p (s c r w)", s=4)
-    o_dram = out.rearrange("(p s) c h w -> p (s c h w)", s=4)
+    out_dram = out.rearrange("(p s) c h w -> p (s c h w)", s=4)
     v_dram = vote_index.rearrange("r w h v -> (r w) (h v)").rearrange(
-        "(j q e) n -> q j (e n)", j=4, e=2
+        "(j q e) n -> q j (e n)", j=PASSES * 2, e=2
     )
-    store_ends = {}
-    pos = 0
-    for cnt in STORES:
-        store_ends[pos + cnt] = pos
-        pos += cnt
+    store_start = {}
+    first = 0
+    for count in STORES:
+        store_start[first + count] = first
+        first += count
 
     with ExitStack() as ctx:
         const = ctx.enter_context(tc.tile_pool(name="const", bufs=1))
         io = ctx.enter_context(tc.tile_pool(name="io", bufs=1))
         work = ctx.enter_context(tc.tile_pool(name="work", bufs=2))
-        tps = ctx.enter_context(tc.psum_pool(name="tps", bufs=1))
-        ops = ctx.enter_context(tc.psum_pool(name="ops", bufs=1))
+        psum = ctx.enter_context(tc.psum_pool(name="psum", bufs=1))
         ctx.enter_context(tc.manual_schedule())
 
         ident = const.tile([P, P], F32, name="ident")
         make_identity(nc, ident[:])
 
+        v_raw = const.tile([P, PASSES * 2, 2 * N], BF16, name="v_raw")
+        nc.sync.dma_start(out=v_raw[:], in_=v_dram)
         x_sb = []
-        for c in range(MT // SLOT):
-            x_sb.append(io.tile([P, SLOT * K], BF16, name="x%d" % c, tag="io%d" % c))
-        o_sb = {}
-        vraw = const.tile([P, 4, 2 * N], BF16, name="vraw")
-        vgrp = const.tile([P, 2, N, 4], BF16, name="vgrp", align_bytes=64)
-        vcodes = const.tile([P, 2 * N], U32, name="vcodes", align_bytes=64)
-        vscl = const.tile([P, 2 * N], U8, name="vscl", align_bytes=64)
-
-        nc.sync.dma_start(out=vraw[:], in_=v_dram)
-        pos = 0
-        for cnt in LOADS:
-            c = pos // SLOT
-            lo = (pos % SLOT) * K
+        for slot in range(ROW_TILES // SLOT):
+            x_sb.append(io.tile([P, SLOT * K], BF16, name="x%d" % slot, tag="io%d" % slot))
+        first = 0
+        for count in LOADS:
+            lo = (first % SLOT) * K
             nc.sync.dma_start(
-                out=x_sb[c][:, lo : lo + cnt * K],
-                in_=x_dram[:, pos * K : (pos + cnt) * K],
+                out=x_sb[first // SLOT][:, lo : lo + count * K],
+                in_=x_dram[:, first * K : (first + count) * K],
             )
-            pos += cnt
+            first += count
 
-        def v_regroup(g, eng_copy):
-            src = vraw[:].rearrange("q j (e n) -> q (j e) n", e=2)[:, 4 * g : 4 * g + 4, :]
-            eng_copy(
-                out=vgrp[:, g].rearrange("q (c i) t -> q c t i", i=4),
-                in_=src.rearrange("q t (c i) -> q c t i", i=4),
+        v_grouped = const.tile([P, PASSES, N, PACK], BF16, name="v_grouped", align_bytes=64)
+        v_codes = const.tile([P, PASSES * N], U32, name="v_codes", align_bytes=64)
+        v_scales = const.tile([P, PASSES * N], U8, name="v_scales", align_bytes=64)
+        v_rows = v_raw[:].rearrange("q j (e n) -> q (j e) n", e=2)
+        for g, copy in ((0, nc.vector.tensor_copy), (1, nc.scalar.copy)):
+            copy(
+                out=v_grouped[:, g].rearrange("q (c i) t -> q c t i", i=4),
+                in_=v_rows[:, PACK * g : PACK * g + PACK, :].rearrange("q t (c i) -> q c t i", i=4),
             )
-
-        def v_quant(g):
+        for g in range(PASSES):
             nc.vector.quantize_mx(
-                out=vcodes[:, N * g : N * g + N].bitcast(FP8X4),
-                scales=vscl[:, N * g : N * g + N],
-                in_=vgrp[:, g].rearrange("q n t -> q (n t)"),
+                out=v_codes[:, N * g : N * g + N].bitcast(FP8X4),
+                scales=v_scales[:, N * g : N * g + N],
+                in_=v_grouped[:, g].rearrange("q n t -> q (n t)"),
             )
 
-        tbs = {}
-        grp = {}
-        cod = {}
-        obs = {}
+        turned = {}
+        x_mx = {}
+        out_sb = {}
 
-        def transposes(i):
-            for b in range(GROUP):
-                m = GROUP * i + b
-                tb = tps.tile([P, 4 * P], F32, name="tb%d" % b, tag="tb%d" % b)
-                tbs[b] = tb
-                xw = x_sb[m // SLOT][:].bitcast(F32)
-                lo = (m % SLOT) * (K // 2)
-                for j in range(4):
-                    sl = 2 * (j % 2) + j // 2
+        def transpose_group(i):
+            for bank in range(GROUP):
+                t = GROUP * i + bank
+                words = x_sb[t // SLOT][:].bitcast(F32)
+                lo = (t % SLOT) * (K // 2)
+                tile = psum.tile([P, PASSES * 2 * P], F32, name="turned%d" % bank, tag="turned%d" % bank)
+                turned[bank] = tile
+                for j in range(PASSES * 2):
+                    place = PASSES * (j % 2) + j // 2
                     nc.tensor.transpose(
-                        tb[:, P * sl : P * sl + P], xw[:, lo + P * j : lo + P * j + P], ident[:]
+                        tile[:, P * place : P * place + P],
+                        words[:, lo + P * j : lo + P * j + P],
+                        ident[:],
                     )
 
-        def exits_t(i, engines):
+        def quantise_group(i):
             grouped = work.tile([P, GROUP * K], BF16, name="grouped", tag="grouped", align_bytes=64)
-            grp[i] = grouped
-            for b in range(GROUP):
-                dst = grouped[:, K * b : K * b + K].rearrange("p (s u e) -> p s u e", u=2, e=2)
-                src = tbs[b][:].bitcast(BF16).rearrange("p (u s e) -> p s u e", u=2, e=2)
-                nc.vector.tensor_scalar_max(out=dst, in0=src, scalar1=0.0)
-
-        def quant(i):
-            codes = work.tile([P, GROUP * 256], U32, name="codes", tag="codes", align_bytes=64)
-            scl = work.tile([P, GROUP * 256], U8, name="scl", tag="scl", align_bytes=64)
-            cod[i] = (codes, scl)
-            nc.vector.quantize_mx(out=codes[:].bitcast(FP8X4), scales=scl[:], in_=grp[i][:])
-
-        def mx(i):
-            codes, scl = cod[i]
-            for b in range(GROUP):
-                ob = ops.tile([P, N], F32, name="ob%d" % b, tag="ob%d" % b)
-                obs[b] = ob
-                for g in range(2):
-                    lo = 256 * b + P * g
-                    nc.tensor.matmul_mx(
-                        out=ob[:],
-                        lhsT=codes[:, lo : lo + P].bitcast(FP8X4),
-                        lhsT_scale=scl[:, lo : lo + P],
-                        rhs=vcodes[:, N * g : N * g + N].bitcast(FP8X4),
-                        rhs_scale=vscl[:, N * g : N * g + N],
-                        start=(g == 0),
-                        stop=(g == 1),
-                    )
-
-        def exits_o(i):
-            for b in range(GROUP):
-                m = GROUP * i + b
-                c = m // SLOT
-                if m % SLOT == 0:
-                    o_sb[c] = io.tile([P, SLOT * N], F32, name="o%d" % c, tag="io%d" % c)
-                lo = (m % SLOT) * N
-                nc.scalar.activation(
-                    out=o_sb[c][:, lo : lo + N], in_=obs[b][:], func=COPY, scale=1.0 / 32.0
+            codes = work.tile([P, GROUP * WORDS], U32, name="codes", tag="codes", align_bytes=64)
+            scales = work.tile([P, GROUP * WORDS], U8, name="scales", tag="scales", align_bytes=64)
+            x_mx[i] = (codes, scales)
+            for bank in range(GROUP):
+                dst = grouped[:, K * bank : K * bank + K].rearrange("p (s u e) -> p s u e", u=2, e=2)
+                src = turned[bank][:].bitcast(BF16).rearrange("p (u s e) -> p s u e", u=2, e=2)
+                if bank == SCALAR_BANK:
+                    nc.scalar.activation(out=dst, in_=src, func=ACT.Relu)
+                else:
+                    nc.vector.tensor_scalar_max(out=dst, in0=src, scalar1=0.0)
+            for half in range(2):
+                lo = half * (GROUP // 2) * WORDS
+                hi = lo + (GROUP // 2) * WORDS
+                nc.vector.quantize_mx(
+                    out=codes[:, lo:hi].bitcast(FP8X4),
+                    scales=scales[:, lo:hi],
+                    in_=grouped[:, PACK * lo : PACK * hi],
                 )
-                if (m + 1) in store_ends:
-                    s0 = store_ends[m + 1]
+
+        def multiply_group(i):
+            codes, scales = x_mx[i]
+            products = []
+            for bank in range(GROUP):
+                product = psum.tile([P, N], F32, name="product%d" % bank, tag="product%d" % bank)
+                products.append(product)
+                for g in range(PASSES):
+                    lo = WORDS * bank + P * g
+                    nc.tensor.matmul_mx(
+                        out=product[:],
+                        lhsT=codes[:, lo : lo + P].bitcast(FP8X4),
+                        lhsT_scale=scales[:, lo : lo + P],
+                        rhs=v_codes[:, N * g : N * g + N].bitcast(FP8X4),
+                        rhs_scale=v_scales[:, N * g : N * g + N],
+                        start=(g == 0),
+                        stop=(g == PASSES - 1),
+                    )
+            for bank in range(GROUP):
+                t = GROUP * i + bank
+                slot = t // SLOT
+                if t % SLOT == 0:
+                    out_sb[slot] = io.tile([P, SLOT * N], F32, name="out%d" % slot, tag="io%d" % slot)
+                hi = (t % SLOT + 1) * N
+                nc.scalar.activation(
+                    out=out_sb[slot][:, hi - N : hi], in_=products[bank][:], func=ACT.Copy, scale=1.0 / 32.0
+                )
+                if t + 1 in store_start:
+                    t0 = store_start[t + 1]
                     nc.sync.dma_start(
-                        out=o_dram[:, s0 * N : (m + 1) * N],
-                        in_=o_sb[c][:, (s0 % SLOT) * N : lo + N],
+                        out=out_dram[:, t0 * N : (t + 1) * N],
+                        in_=out_sb[slot][:, (t0 % SLOT) * N : hi],
                     )
 
-        v_regroup(0, nc.vector.tensor_copy)
-        v_regroup(1, nc.scalar.copy)
-        v_quant(0)
-        v_quant(1)
-        transposes(0)
-        exits_t(0, "vvvv")
-        quant(0)
-        for i in range(NG):
-            if i + 1 < NG:
-                transposes(i + 1)
-                exits_t(i + 1, "vvvv")
-                quant(i + 1)
-            mx(i)
-            exits_o(i)
+        transpose_group(0)
+        quantise_group(0)
+        for i in range(GROUPS):
+            if i + 1 < GROUPS:
+                transpose_group(i + 1)
+                quantise_group(i + 1)
+            multiply_group(i)

from contextlib import ExitStack

import concourse.mybir as mybir
from concourse.masks import make_identity

BF16 = mybir.dt.bfloat16
F32 = mybir.dt.float32
U32 = mybir.dt.uint32
U8 = mybir.dt.uint8
FP8X4 = mybir.dt.float8_e4m3fn_x4
ACT = mybir.ActivationFunctionType

P = 128
M = 8192
K = 1024
N = 512
FLOPS = 2 * M * K * N

PACK = 4
PASSES = K // (P * PACK)
WORDS = K // PACK
ROW_TILES = M // P
GROUP = 4
GROUPS = ROW_TILES // GROUP
SLOT = 8
LOADS = [2, 2, 4, 4, 4, 8, 8, 8, 8, 8, 8]
STORES = [8, 8, 8, 8, 8, 4, 4, 4, 4, 4, 2, 2]
SCALAR_BANK = 1


def tile_ht_t_kernel(tc, image, vote_index, out):
    nc = tc.nc
    x_dram = image.rearrange("(p s) c r w -> p (s c r w)", s=4)
    out_dram = out.rearrange("(p s) c h w -> p (s c h w)", s=4)
    v_dram = vote_index.rearrange("r w h v -> (r w) (h v)").rearrange(
        "(j q e) n -> q j (e n)", j=PASSES * 2, e=2
    )
    store_start = {}
    first = 0
    for count in STORES:
        store_start[first + count] = first
        first += count

    with ExitStack() as ctx:
        const = ctx.enter_context(tc.tile_pool(name="const", bufs=1))
        io = ctx.enter_context(tc.tile_pool(name="io", bufs=1))
        work = ctx.enter_context(tc.tile_pool(name="work", bufs=2))
        psum = ctx.enter_context(tc.psum_pool(name="psum", bufs=1))
        ctx.enter_context(tc.manual_schedule())

        ident = const.tile([P, P], F32, name="ident")
        make_identity(nc, ident[:])

        v_raw = const.tile([P, PASSES * 2, 2 * N], BF16, name="v_raw")
        nc.sync.dma_start(out=v_raw[:], in_=v_dram)
        x_sb = []
        for slot in range(ROW_TILES // SLOT):
            x_sb.append(io.tile([P, SLOT * K], BF16, name="x%d" % slot, tag="io%d" % slot))
        first = 0
        for count in LOADS:
            lo = (first % SLOT) * K
            nc.sync.dma_start(
                out=x_sb[first // SLOT][:, lo : lo + count * K],
                in_=x_dram[:, first * K : (first + count) * K],
            )
            first += count

        v_grouped = const.tile([P, PASSES, N, PACK], BF16, name="v_grouped", align_bytes=64)
        v_codes = const.tile([P, PASSES * N], U32, name="v_codes", align_bytes=64)
        v_scales = const.tile([P, PASSES * N], U8, name="v_scales", align_bytes=64)
        v_rows = v_raw[:].rearrange("q j (e n) -> q (j e) n", e=2)
        for g, copy in ((0, nc.vector.tensor_copy), (1, nc.scalar.copy)):
            copy(
                out=v_grouped[:, g].rearrange("q (c i) t -> q c t i", i=4),
                in_=v_rows[:, PACK * g : PACK * g + PACK, :].rearrange("q t (c i) -> q c t i", i=4),
            )
        for g in range(PASSES):
            nc.vector.quantize_mx(
                out=v_codes[:, N * g : N * g + N].bitcast(FP8X4),
                scales=v_scales[:, N * g : N * g + N],
                in_=v_grouped[:, g].rearrange("q n t -> q (n t)"),
            )

        turned = {}
        x_mx = {}
        out_sb = {}

        def transpose_group(i):
            for bank in range(GROUP):
                t = GROUP * i + bank
                words = x_sb[t // SLOT][:].bitcast(F32)
                lo = (t % SLOT) * (K // 2)
                tile = psum.tile([P, PASSES * 2 * P], F32, name="turned%d" % bank, tag="turned%d" % bank)
                turned[bank] = tile
                for j in range(PASSES * 2):
                    place = PASSES * (j % 2) + j // 2
                    nc.tensor.transpose(
                        tile[:, P * place : P * place + P],
                        words[:, lo + P * j : lo + P * j + P],
                        ident[:],
                    )

        def quantise_group(i):
            grouped = work.tile([P, GROUP * K], BF16, name="grouped", tag="grouped", align_bytes=64)
            codes = work.tile([P, GROUP * WORDS], U32, name="codes", tag="codes", align_bytes=64)
            scales = work.tile([P, GROUP * WORDS], U8, name="scales", tag="scales", align_bytes=64)
            x_mx[i] = (codes, scales)
            for bank in range(GROUP):
                dst = grouped[:, K * bank : K * bank + K].rearrange("p (s u e) -> p s u e", u=2, e=2)
                src = turned[bank][:].bitcast(BF16).rearrange("p (u s e) -> p s u e", u=2, e=2)
                if bank == SCALAR_BANK:
                    nc.scalar.activation(out=dst, in_=src, func=ACT.Relu)
                else:
                    nc.vector.tensor_scalar_max(out=dst, in0=src, scalar1=0.0)
            for half in range(2):
                lo = half * (GROUP // 2) * WORDS
                hi = lo + (GROUP // 2) * WORDS
                nc.vector.quantize_mx(
                    out=codes[:, lo:hi].bitcast(FP8X4),
                    scales=scales[:, lo:hi],
                    in_=grouped[:, PACK * lo : PACK * hi],
                )

        def multiply_group(i):
            codes, scales = x_mx[i]
            products = []
            for bank in range(GROUP):
                product = psum.tile([P, N], F32, name="product%d" % bank, tag="product%d" % bank)
                products.append(product)
                for g in range(PASSES):
                    lo = WORDS * bank + P * g
                    nc.tensor.matmul_mx(
                        out=product[:],
                        lhsT=codes[:, lo : lo + P].bitcast(FP8X4),
                        lhsT_scale=scales[:, lo : lo + P],
                        rhs=v_codes[:, N * g : N * g + N].bitcast(FP8X4),
                        rhs_scale=v_scales[:, N * g : N * g + N],
                        start=(g == 0),
                        stop=(g == PASSES - 1),
                    )
            for bank in range(GROUP):
                t = GROUP * i + bank
                slot = t // SLOT
                if t % SLOT == 0:
                    out_sb[slot] = io.tile([P, SLOT * N], F32, name="out%d" % slot, tag="io%d" % slot)
                hi = (t % SLOT + 1) * N
                nc.scalar.activation(
                    out=out_sb[slot][:, hi - N : hi], in_=products[bank][:], func=ACT.Copy, scale=1.0 / 32.0
                )
                if t + 1 in store_start:
                    t0 = store_start[t + 1]
                    nc.sync.dma_start(
                        out=out_dram[:, t0 * N : (t + 1) * N],
                        in_=out_sb[slot][:, (t0 % SLOT) * N : hi],
                    )

        transpose_group(0)
        quantise_group(0)
        for i in range(GROUPS):
            if i + 1 < GROUPS:
                transpose_group(i + 1)
                quantise_group(i + 1)
            multiply_group(i)
